import numpy as np
import ml_dtypes


def mxq(x, axis, fmt="e4m3"):
    dtype, down = {"e4m3": (ml_dtypes.float8_e4m3fn, 7), "e5m2": (ml_dtypes.float8_e5m2, 14)}[fmt]
    v = np.moveaxis(np.asarray(x, np.float32).astype(ml_dtypes.bfloat16).astype(np.float64), axis, -1)
    blocks = v.reshape(v.shape[:-1] + (-1, 32))
    amax = np.abs(blocks).max(-1, keepdims=True)
    byte = np.maximum(np.where(amax > 0, np.frexp(amax)[1] - 1 + 127, 0) - down, 1)
    scale = np.exp2(byte - 127.0)
    codes = (blocks / scale).astype(np.float32).astype(dtype).astype(np.float64)
    return np.moveaxis((codes * scale).reshape(v.shape), -1, axis)


WIDE = False


def mx_kscale(k):
    if not WIDE:
        return np.ones(k)
    levels = np.array([20, -20, 10, -10, 0])
    a = np.random.permutation(np.resize(levels, k // 512 * 4)).reshape(k // 512, 4)
    idx = np.arange(k)
    return np.exp2(a[idx // 512, idx % 128 // 32])


BF16 = ml_dtypes.bfloat16


def bf(x):
    return np.asarray(x, np.float32).astype(BF16)


def f64(x):
    return np.asarray(x).astype(np.float64)


B, N, D, C = 2048, 2048, 512, 8

SIGMA = 1.0


def setup_inputs():
    s = mx_kscale(N)
    centres = (0.8 * np.random.standard_normal((1, D)) + 0.9 * np.random.standard_normal((C, D))) / np.sqrt(D)

    def draw(rows):
        amp = 0.5 + np.random.random((rows, 1))
        return bf(centres[np.random.randint(0, C, rows)] * amp + np.random.standard_normal((rows, D)) * 0.7 / np.sqrt(D))

    x0 = draw(B)
    t0 = draw(N)
    g = bf(np.random.standard_normal((B, N)) * np.exp2(np.random.randint(-12, 1, (B, 1))) * 16.0 * s[None, :])
    xf, tf = f64(x0), f64(t0)
    dist = np.sum(xf * xf, axis=-1, keepdims=True) + np.sum(tf * tf, axis=-1)[None, :] - 2.0 * (xf @ tf.T)
    return {"inputs": bf(xf / np.max(s)), "train_data": bf(tf / s[:, None]), "dist": np.asarray(dist, np.float32), "grad_out": g}


def reference(inputs, train_data, dist, grad_out):
    x, t, z = f64(inputs), f64(train_data), f64(dist)
    p = np.where(z > 0.0, np.exp(-np.maximum(z, 0.0) / (2.0 * SIGMA ** 2)), 0.0)
    e = f64(grad_out) * p / SIGMA ** 2
    r = np.sum(e, axis=1, keepdims=True)
    return (mxq(e, 1, "e5m2") @ mxq(t, 0, "e4m3")) - x * r

@@ -1,0 +1,166 @@
+from contextlib import ExitStack
+
+import concourse.mybir as mybir
+from concourse.masks import make_identity
+
+F32 = mybir.dt.float32
+BF16 = mybir.dt.bfloat16
+U32 = mybir.dt.uint32
+U8 = mybir.dt.uint8
+E5M2X4 = mybir.dt.float8_e5m2_x4
+E4M3X4 = mybir.dt.float8_e4m3fn_x4
+ALU = mybir.AluOpType
+ACT = mybir.ActivationFunctionType
+
+P = 128
+B = 2048
+N = 2048
+D = 512
+ROW_TILES = B // P
+K_PASS = 4 * P
+PASSES = N // K_PASS
+AHEAD = 3
+EXP_CAP = 3.0e38
+
+FLOPS = 2 * B * N * D
+
+
+def tile_patternlayer_t_v_kernel(tc, inputs, train_data, dist, grad_out, out):
+    nc = tc.nc
+
+    dist_tiles = dist.rearrange("(p i) n -> i p n", i=ROW_TILES)
+    grad_tiles = grad_out.rearrange("(p i) n -> i p n", i=ROW_TILES)
+    x_tiles = inputs.rearrange("(p i) d -> i p d", i=ROW_TILES)
+    out_tiles = out.rearrange("(p i) d -> i p d", i=ROW_TILES)
+    train_passes = train_data.rearrange("(c u p e) d -> c p u (e d)", c=PASSES, u=2, p=P, e=2)
+
+    with ExitStack() as stack:
+        stack.enter_context(tc.manual_schedule())
+        keep = stack.enter_context(tc.tile_pool(name="keep", bufs=1))
+        loads = stack.enter_context(tc.tile_pool(name="loads", bufs=AHEAD + 1))
+        x_pool = stack.enter_context(tc.tile_pool(name="x_pool", bufs=AHEAD + 3))
+        stage = stack.enter_context(tc.tile_pool(name="stage", bufs=2))
+        small = stack.enter_context(tc.tile_pool(name="small", bufs=3))
+        flipped = stack.enter_context(tc.psum_pool(name="flipped", bufs=4))
+        sums = stack.enter_context(tc.psum_pool(name="sums", bufs=2))
+
+        z_of, g_of, x_of, prob_of, e_of, r_of, neg_r_of = {}, {}, {}, {}, {}, {}, {}
+        banks_of, grouped_of, codes_of, scales_of, acc_of = {}, {}, {}, {}, {}
+
+        def load(i):
+            z = loads.tile([P, N], F32)
+            nc.sync.dma_start(out=z[:], in_=dist_tiles[i])
+            g = loads.tile([P, N], BF16)
+            nc.sync.dma_start(out=g[:], in_=grad_tiles[i])
+            x = x_pool.tile([P, D], BF16)
+            nc.sync.dma_start(out=x[:], in_=x_tiles[i])
+            z_of[i], g_of[i], x_of[i] = z, g, x
+
+        def exponential(i):
+            prob = stage.tile([P, N], F32)
+            nc.scalar.activation(out=prob[:], in_=z_of[i][:], func=ACT.Exp, scale=-0.5)
+            prob_of[i] = prob
+
+        def weigh(i):
+            g_kept = stage.tile([P, N], BF16)
+            nc.vector.scalar_tensor_tensor(
+                out=g_kept[:], in0=z_of[i][:], scalar=0.0, in1=g_of[i][:], op0=ALU.is_gt, op1=ALU.mult
+            )
+            e = stage.tile([P, N], BF16)
+            r = small.tile([P, 1], F32)
+            nc.vector.scalar_tensor_tensor(
+                out=e[:], in0=prob_of[i][:], scalar=EXP_CAP, in1=g_kept[:], op0=ALU.min, op1=ALU.mult, accum_out=r[:]
+            )
+            e_of[i], r_of[i] = e, r
+
+        def flip(i):
+            e_words = e_of[i][:].bitcast(F32)
+            banks_of[i] = []
+            for h in range(PASSES // 2):
+                bank = flipped.tile([P, 2, 2, P], F32)
+                for c in range(2):
+                    for u in range(2):
+                        w0 = P * (4 * h + 2 * c + u)
+                        nc.tensor.transpose(bank[:, c, u, :], e_words[:, w0 : w0 + P], identity[:])
+                banks_of[i].append(bank)
+
+        def regroup(i):
+            e_grouped = stage.tile([P, PASSES, P, 4], BF16, align_bytes=64)
+            e_grouped_words = e_grouped[:].bitcast(F32)
+            for h in range(PASSES // 2):
+                nc.scalar.copy(
+                    out=e_grouped_words[:, 2 * h : 2 * h + 2, :, :],
+                    in_=banks_of[i][h][:].rearrange("p c u b -> p c b u"),
+                )
+            neg_r = small.tile([P, 1], F32)
+            nc.scalar.mul(out=neg_r[:], in_=r_of[i][:], mul=-1.0)
+            grouped_of[i], neg_r_of[i] = e_grouped, neg_r
+
+        def quantise(i):
+            e_codes = stage.tile([P, PASSES, P], U32, align_bytes=64)
+            e_scales = stage.tile([P, PASSES, P], U8, align_bytes=64)
+            nc.vector.quantize_mx(
+                out=e_codes[:].rearrange("p c b -> p (c b)").bitcast(E5M2X4),
+                scales=e_scales[:].rearrange("p c b -> p (c b)"),
+                in_=grouped_of[i][:].rearrange("p c b t -> p (c b t)"),
+            )
+            codes_of[i], scales_of[i] = e_codes, e_scales
+
+        def multiply(i):
+            acc = sums.tile([P, D], F32)
+            for c in range(PASSES):
+                nc.tensor.matmul_mx(
+                    out=acc[:],
+                    lhsT=codes_of[i][:, c, :].bitcast(E5M2X4),
+                    lhsT_scale=scales_of[i][:, c, :],
+                    rhs=t_codes[:, c, :].bitcast(E4M3X4),
+                    rhs_scale=t_scales[:, c, :],
+                    start=(c == 0),
+                    stop=(c == PASSES - 1),
+                )
+            acc_of[i] = acc
+
+        def finish(i):
+            result = stage.tile([P, D], F32)
+            nc.vector.scalar_tensor_tensor(
+                out=result[:], in0=x_of[i][:], scalar=neg_r_of[i][:, 0:1], in1=acc_of[i][:], op0=ALU.mult, op1=ALU.add
+            )
+            nc.sync.dma_start(out=out_tiles[i], in_=result[:])
+
+        identity = keep.tile([P, P], F32)
+        make_identity(nc, identity[:])
+
+        t_raw = keep.tile([P, PASSES, 4, D], BF16)
+        t_grouped = keep.tile([P, PASSES, D, 4], BF16, align_bytes=64)
+        t_codes = keep.tile([P, PASSES, D], U32, align_bytes=64)
+        t_scales = keep.tile([P, PASSES, D], U8, align_bytes=64)
+        for c in range(PASSES):
+            nc.sync.dma_start(out=t_raw[:, c].rearrange("p (u e) d -> p u (e d)", u=2), in_=train_passes[c])
+        for i in range(AHEAD):
+            load(i)
+        for c in range(PASSES):
+            copy_engine = nc.vector.tensor_copy if c % 2 == 0 else nc.scalar.copy
+            copy_engine(out=t_grouped[:, c], in_=t_raw[:, c].rearrange("p t d -> p d t"))
+        for c in range(PASSES):
+            nc.vector.quantize_mx(
+                out=t_codes[:, c, :].bitcast(E4M3X4),
+                scales=t_scales[:, c, :],
+                in_=t_grouped[:, c].rearrange("p d t -> p (d t)"),
+            )
+
+        exponential(0)
+        for s in range(ROW_TILES + 2):
+            if s + AHEAD < ROW_TILES:
+                load(s + AHEAD)
+            if 1 <= s <= ROW_TILES:
+                regroup(s - 1)
+            if s + 1 < ROW_TILES:
+                exponential(s + 1)
+            if s < ROW_TILES:
+                weigh(s)
+                flip(s)
+            if 1 <= s <= ROW_TILES:
+                quantise(s - 1)
+                multiply(s - 1)
+            if s >= 2:
+                finish(s - 2)

@@ -20,6 +20,8 @@ ROW_TILES = B // P
 K_PASS = 4 * P
 PASSES = N // K_PASS
 AHEAD = 3
+QUANTISE_LAG = 2
+FINISH_LAG = 4
 EXP_CAP = 3.0e38
 
 FLOPS = 2 * B * N * D
@@ -38,14 +40,15 @@ def tile_patternlayer_t_v_kernel(tc, inputs, train_data, dist, grad_out, out):
         stack.enter_context(tc.manual_schedule())
         keep = stack.enter_context(tc.tile_pool(name="keep", bufs=1))
         loads = stack.enter_context(tc.tile_pool(name="loads", bufs=AHEAD + 1))
-        x_pool = stack.enter_context(tc.tile_pool(name="x_pool", bufs=AHEAD + 3))
+        x_pool = stack.enter_context(tc.tile_pool(name="x_pool", bufs=AHEAD + FINISH_LAG + 1))
         stage = stack.enter_context(tc.tile_pool(name="stage", bufs=2))
-        small = stack.enter_context(tc.tile_pool(name="small", bufs=3))
+        waiting = stack.enter_context(tc.tile_pool(name="waiting", bufs=QUANTISE_LAG + 1))
+        small = stack.enter_context(tc.tile_pool(name="small", bufs=FINISH_LAG + 1))
         flipped = stack.enter_context(tc.psum_pool(name="flipped", bufs=4))
-        sums = stack.enter_context(tc.psum_pool(name="sums", bufs=2))
+        sums = stack.enter_context(tc.psum_pool(name="sums", bufs=FINISH_LAG - QUANTISE_LAG + 1))
 
         z_of, g_of, x_of, prob_of, e_of, r_of, neg_r_of = {}, {}, {}, {}, {}, {}, {}
-        banks_of, grouped_of, codes_of, scales_of, acc_of = {}, {}, {}, {}, {}
+        banks_of, grouped_of, codes_of, scales_of, acc_of, g_kept_of = {}, {}, {}, {}, {}, {}
 
         def load(i):
             z = loads.tile([P, N], F32)
@@ -61,15 +64,18 @@ def tile_patternlayer_t_v_kernel(tc, inputs, train_data, dist, grad_out, out):
             nc.scalar.activation(out=prob[:], in_=z_of[i][:], func=ACT.Exp, scale=-0.5)
             prob_of[i] = prob
 
-        def weigh(i):
+        def mask(i):
             g_kept = stage.tile([P, N], BF16)
             nc.vector.scalar_tensor_tensor(
                 out=g_kept[:], in0=z_of[i][:], scalar=0.0, in1=g_of[i][:], op0=ALU.is_gt, op1=ALU.mult
             )
+            g_kept_of[i] = g_kept
+
+        def weigh(i):
             e = stage.tile([P, N], BF16)
             r = small.tile([P, 1], F32)
             nc.vector.scalar_tensor_tensor(
-                out=e[:], in0=prob_of[i][:], scalar=EXP_CAP, in1=g_kept[:], op0=ALU.min, op1=ALU.mult, accum_out=r[:]
+                out=e[:], in0=prob_of[i][:], scalar=EXP_CAP, in1=g_kept_of[i][:], op0=ALU.min, op1=ALU.mult, accum_out=r[:]
             )
             e_of[i], r_of[i] = e, r
 
@@ -85,7 +91,7 @@ def tile_patternlayer_t_v_kernel(tc, inputs, train_data, dist, grad_out, out):
                 banks_of[i].append(bank)
 
         def regroup(i):
-            e_grouped = stage.tile([P, PASSES, P, 4], BF16, align_bytes=64)
+            e_grouped = waiting.tile([P, PASSES, P, 4], BF16, align_bytes=64)
             e_grouped_words = e_grouped[:].bitcast(F32)
             for h in range(PASSES // 2):
                 nc.scalar.copy(
@@ -149,18 +155,20 @@ def tile_patternlayer_t_v_kernel(tc, inputs, train_data, dist, grad_out, out):
             )
 
         exponential(0)
-        for s in range(ROW_TILES + 2):
+        mask(0)
+        for s in range(ROW_TILES + FINISH_LAG):
             if s + AHEAD < ROW_TILES:
                 load(s + AHEAD)
             if 1 <= s <= ROW_TILES:
                 regroup(s - 1)
             if s + 1 < ROW_TILES:
                 exponential(s + 1)
+                mask(s + 1)
             if s < ROW_TILES:
                 weigh(s)
                 flip(s)
-            if 1 <= s <= ROW_TILES:
-                quantise(s - 1)
-                multiply(s - 1)
-            if s >= 2:
-                finish(s - 2)
+            if 0 <= s - QUANTISE_LAG < ROW_TILES:
+                quantise(s - QUANTISE_LAG)
+                multiply(s - QUANTISE_LAG)
+            if s >= FINISH_LAG:
+                finish(s - FINISH_LAG)

@@ -20,8 +20,8 @@ ROW_TILES = B // P
 K_PASS = 4 * P
 PASSES = N // K_PASS
 AHEAD = 3
-QUANTISE_LAG = 2
-FINISH_LAG = 4
+QUANTISE_LAG = 1
+FINISH_LAG = 6
 EXP_CAP = 3.0e38
 
 FLOPS = 2 * B * N * D
@@ -44,7 +44,8 @@ def tile_patternlayer_t_v_kernel(tc, inputs, train_data, dist, grad_out, out):
         stage = stack.enter_context(tc.tile_pool(name="stage", bufs=2))
         waiting = stack.enter_context(tc.tile_pool(name="waiting", bufs=QUANTISE_LAG + 1))
         small = stack.enter_context(tc.tile_pool(name="small", bufs=FINISH_LAG + 1))
-        flipped = stack.enter_context(tc.psum_pool(name="flipped", bufs=4))
+        results = stack.enter_context(tc.tile_pool(name="results", bufs=FINISH_LAG))
+        flipped = stack.enter_context(tc.psum_pool(name="flipped", bufs=2))
         sums = stack.enter_context(tc.psum_pool(name="sums", bufs=FINISH_LAG - QUANTISE_LAG + 1))
 
         z_of, g_of, x_of, prob_of, e_of, r_of, neg_r_of = {}, {}, {}, {}, {}, {}, {}
@@ -127,7 +128,7 @@ def tile_patternlayer_t_v_kernel(tc, inputs, train_data, dist, grad_out, out):
             acc_of[i] = acc
 
         def finish(i):
-            result = stage.tile([P, D], F32)
+            result = results.tile([P, D], F32)
             nc.vector.scalar_tensor_tensor(
                 out=result[:], in0=x_of[i][:], scalar=neg_r_of[i][:, 0:1], in1=acc_of[i][:], op0=ALU.mult, op1=ALU.add
             )
@@ -163,12 +164,13 @@ def tile_patternlayer_t_v_kernel(tc, inputs, train_data, dist, grad_out, out):
                 regroup(s - 1)
             if s + 1 < ROW_TILES:
                 exponential(s + 1)
-                mask(s + 1)
             if s < ROW_TILES:
                 weigh(s)
                 flip(s)
+            if s + 1 < ROW_TILES:
+                mask(s + 1)
+            if s >= FINISH_LAG:
+                finish(s - FINISH_LAG)
             if 0 <= s - QUANTISE_LAG < ROW_TILES:
                 quantise(s - QUANTISE_LAG)
                 multiply(s - QUANTISE_LAG)
-            if s >= FINISH_LAG:
-                finish(s - FINISH_LAG)

@@ -22,6 +22,7 @@ PASSES = N // K_PASS
 AHEAD = 3
 QUANTISE_LAG = 1
 FINISH_LAG = 6
+SIGN_COLUMNS = 1536
 EXP_CAP = 3.0e38
 
 FLOPS = 2 * B * N * D
@@ -44,12 +45,14 @@ def tile_patternlayer_t_v_kernel(tc, inputs, train_data, dist, grad_out, out):
         stage = stack.enter_context(tc.tile_pool(name="stage", bufs=2))
         waiting = stack.enter_context(tc.tile_pool(name="waiting", bufs=QUANTISE_LAG + 1))
         small = stack.enter_context(tc.tile_pool(name="small", bufs=FINISH_LAG + 1))
+        signs = stack.enter_context(tc.tile_pool(name="signs", bufs=3))
         results = stack.enter_context(tc.tile_pool(name="results", bufs=FINISH_LAG))
         flipped = stack.enter_context(tc.psum_pool(name="flipped", bufs=2))
         sums = stack.enter_context(tc.psum_pool(name="sums", bufs=FINISH_LAG - QUANTISE_LAG + 1))
 
-        z_of, g_of, x_of, prob_of, e_of, r_of, neg_r_of = {}, {}, {}, {}, {}, {}, {}
+        z_of, g_of, x_of, prob_of, e_of, r_of = {}, {}, {}, {}, {}, {}
         banks_of, grouped_of, codes_of, scales_of, acc_of, g_kept_of = {}, {}, {}, {}, {}, {}
+        z_sign_of = {}
 
         def load(i):
             z = loads.tile([P, N], F32)
@@ -65,10 +68,25 @@ def tile_patternlayer_t_v_kernel(tc, inputs, train_data, dist, grad_out, out):
             nc.scalar.activation(out=prob[:], in_=z_of[i][:], func=ACT.Exp, scale=-0.5)
             prob_of[i] = prob
 
+        def sign(i):
+            z_sign = signs.tile([P, SIGN_COLUMNS], BF16)
+            nc.scalar.activation(out=z_sign[:], in_=z_of[i][:, :SIGN_COLUMNS], func=ACT.Sign)
+            z_sign_of[i] = z_sign
+
         def mask(i):
             g_kept = stage.tile([P, N], BF16)
+            z_sign = z_sign_of[i]
+            nc.vector.tensor_scalar_max(out=z_sign[:], in0=z_sign[:], scalar1=0.0)
             nc.vector.scalar_tensor_tensor(
-                out=g_kept[:], in0=z_of[i][:], scalar=0.0, in1=g_of[i][:], op0=ALU.is_gt, op1=ALU.mult
+                out=g_kept[:, SIGN_COLUMNS:],
+                in0=z_of[i][:, SIGN_COLUMNS:],
+                scalar=0.0,
+                in1=g_of[i][:, SIGN_COLUMNS:],
+                op0=ALU.is_gt,
+                op1=ALU.mult,
+            )
+            nc.vector.tensor_tensor(
+                out=g_kept[:, :SIGN_COLUMNS], in0=z_sign[:], in1=g_of[i][:, :SIGN_COLUMNS], op=ALU.mult
             )
             g_kept_of[i] = g_kept
 
@@ -99,9 +117,7 @@ def tile_patternlayer_t_v_kernel(tc, inputs, train_data, dist, grad_out, out):
                     out=e_grouped_words[:, 2 * h : 2 * h + 2, :, :],
                     in_=banks_of[i][h][:].rearrange("p c u b -> p c b u"),
                 )
-            neg_r = small.tile([P, 1], F32)
-            nc.scalar.mul(out=neg_r[:], in_=r_of[i][:], mul=-1.0)
-            grouped_of[i], neg_r_of[i] = e_grouped, neg_r
+            grouped_of[i] = e_grouped
 
         def quantise(i):
             e_codes = stage.tile([P, PASSES, P], U32, align_bytes=64)
@@ -130,7 +146,13 @@ def tile_patternlayer_t_v_kernel(tc, inputs, train_data, dist, grad_out, out):
         def finish(i):
             result = results.tile([P, D], F32)
             nc.vector.scalar_tensor_tensor(
-                out=result[:], in0=x_of[i][:], scalar=neg_r_of[i][:, 0:1], in1=acc_of[i][:], op0=ALU.mult, op1=ALU.add
+                out=result[:],
+                in0=x_of[i][:],
+                scalar=r_of[i][:, 0:1],
+                in1=acc_of[i][:],
+                op0=ALU.mult,
+                op1=ALU.subtract,
+                reverse1=True,
             )
             nc.sync.dma_start(out=out_tiles[i], in_=result[:])
 
@@ -146,8 +168,7 @@ def tile_patternlayer_t_v_kernel(tc, inputs, train_data, dist, grad_out, out):
         for i in range(AHEAD):
             load(i)
         for c in range(PASSES):
-            copy_engine = nc.vector.tensor_copy if c % 2 == 0 else nc.scalar.copy
-            copy_engine(out=t_grouped[:, c], in_=t_raw[:, c].rearrange("p t d -> p d t"))
+            nc.vector.tensor_copy(out=t_grouped[:, c], in_=t_raw[:, c].rearrange("p t d -> p d t"))
         for c in range(PASSES):
             nc.vector.quantize_mx(
                 out=t_codes[:, c, :].bitcast(E4M3X4),
@@ -155,7 +176,9 @@ def tile_patternlayer_t_v_kernel(tc, inputs, train_data, dist, grad_out, out):
                 in_=t_grouped[:, c].rearrange("p d t -> p (d t)"),
             )
 
+        sign(0)
         exponential(0)
+        sign(1)
         mask(0)
         for s in range(ROW_TILES + FINISH_LAG):
             if s + AHEAD < ROW_TILES:
@@ -164,6 +187,8 @@ def tile_patternlayer_t_v_kernel(tc, inputs, train_data, dist, grad_out, out):
                 regroup(s - 1)
             if s + 1 < ROW_TILES:
                 exponential(s + 1)
+            if s + 2 < ROW_TILES:
+                sign(s + 2)
             if s < ROW_TILES:
                 weigh(s)
                 flip(s)

@@ -23,6 +23,7 @@ AHEAD = 3
 QUANTISE_LAG = 1
 FINISH_LAG = 6
 SIGN_COLUMNS = 1536
+UNSIGNED_TILES = 2
 EXP_CAP = 3.0e38
 
 FLOPS = 2 * B * N * D
@@ -54,24 +55,45 @@ def tile_patternlayer_t_v_kernel(tc, inputs, train_data, dist, grad_out, out):
         banks_of, grouped_of, codes_of, scales_of, acc_of, g_kept_of = {}, {}, {}, {}, {}, {}
         z_sign_of = {}
 
-        def load(i):
+        def load(i, parts=1):
             z = loads.tile([P, N], F32)
-            nc.sync.dma_start(out=z[:], in_=dist_tiles[i])
             g = loads.tile([P, N], BF16)
-            nc.sync.dma_start(out=g[:], in_=grad_tiles[i])
+            for h in range(parts):
+                cols = slice(h * (N // parts), (h + 1) * (N // parts))
+                nc.sync.dma_start(out=z[:, cols], in_=dist_tiles[i][:, cols])
+                nc.sync.dma_start(out=g[:, cols], in_=grad_tiles[i][:, cols])
+            z_of[i], g_of[i] = z, g
+
+        def load_x(i):
             x = x_pool.tile([P, D], BF16)
             nc.sync.dma_start(out=x[:], in_=x_tiles[i])
-            z_of[i], g_of[i], x_of[i] = z, g, x
+            x_of[i] = x
 
-        def exponential(i):
+        def exponential(i, parts=1):
             prob = stage.tile([P, N], F32)
-            nc.scalar.activation(out=prob[:], in_=z_of[i][:], func=ACT.Exp, scale=-0.5)
+            for h in range(parts):
+                cols = slice(h * (N // parts), (h + 1) * (N // parts))
+                nc.scalar.activation(out=prob[:, cols], in_=z_of[i][:, cols], func=ACT.Exp, scale=-0.5)
             prob_of[i] = prob
 
         def sign(i):
             z_sign = signs.tile([P, SIGN_COLUMNS], BF16)
             nc.scalar.activation(out=z_sign[:], in_=z_of[i][:, :SIGN_COLUMNS], func=ACT.Sign)
             z_sign_of[i] = z_sign
+
+        def mask_on_vector(i, parts):
+            g_kept = stage.tile([P, N], BF16)
+            for h in range(parts):
+                cols = slice(h * (N // parts), (h + 1) * (N // parts))
+                nc.vector.scalar_tensor_tensor(
+                    out=g_kept[:, cols],
+                    in0=z_of[i][:, cols],
+                    scalar=0.0,
+                    in1=g_of[i][:, cols],
+                    op0=ALU.is_gt,
+                    op1=ALU.mult,
+                )
+            g_kept_of[i] = g_kept
 
         def mask(i):
             g_kept = stage.tile([P, N], BF16)
@@ -163,37 +185,62 @@ def tile_patternlayer_t_v_kernel(tc, inputs, train_data, dist, grad_out, out):
         t_grouped = keep.tile([P, PASSES, D, 4], BF16, align_bytes=64)
         t_codes = keep.tile([P, PASSES, D], U32, align_bytes=64)
         t_scales = keep.tile([P, PASSES, D], U8, align_bytes=64)
-        for c in range(PASSES):
+        def load_train(c):
             nc.sync.dma_start(out=t_raw[:, c].rearrange("p (u e) d -> p u (e d)", u=2), in_=train_passes[c])
-        for i in range(AHEAD):
-            load(i)
-        for c in range(PASSES):
-            nc.vector.tensor_copy(out=t_grouped[:, c], in_=t_raw[:, c].rearrange("p t d -> p d t"))
-        for c in range(PASSES):
+
+        def regroup_train(engine_copy, c):
+            engine_copy(out=t_grouped[:, c], in_=t_raw[:, c].rearrange("p t d -> p d t"))
+
+        def quantise_train(c):
             nc.vector.quantize_mx(
                 out=t_codes[:, c, :].bitcast(E4M3X4),
                 scales=t_scales[:, c, :],
                 in_=t_grouped[:, c].rearrange("p d t -> p (d t)"),
             )
 
-        sign(0)
-        exponential(0)
-        sign(1)
-        mask(0)
+        load_train(0)
+        load_train(1)
+        load(0, parts=2)
+        load_train(2)
+        load(1)
+        load_train(3)
+        load(2)
+        for i in range(AHEAD):
+            load_x(i)
+
+        regroup_train(nc.vector.tensor_copy, 0)
+        regroup_train(nc.vector.tensor_copy, 1)
+        quantise_train(0)
+        quantise_train(1)
+        exponential(0, parts=2)
+        mask_on_vector(0, parts=2)
+        regroup_train(nc.scalar.copy, 2)
         for s in range(ROW_TILES + FINISH_LAG):
             if s + AHEAD < ROW_TILES:
                 load(s + AHEAD)
+                load_x(s + AHEAD)
+            if s == 0:
+                exponential(1)
             if 1 <= s <= ROW_TILES:
                 regroup(s - 1)
-            if s + 1 < ROW_TILES:
+            if s == 0:
+                regroup_train(nc.scalar.copy, 3)
+            if 1 <= s and s + 1 < ROW_TILES:
                 exponential(s + 1)
             if s + 2 < ROW_TILES:
                 sign(s + 2)
             if s < ROW_TILES:
                 weigh(s)
                 flip(s)
+            if s == 0:
+                quantise_train(2)
             if s + 1 < ROW_TILES:
-                mask(s + 1)
+                if s + 1 < UNSIGNED_TILES:
+                    mask_on_vector(s + 1, parts=1)
+                else:
+                    mask(s + 1)
+            if s == 1:
+                quantise_train(3)
             if s >= FINISH_LAG:
                 finish(s - FINISH_LAG)
             if 0 <= s - QUANTISE_LAG < ROW_TILES:

@@ -21,8 +21,9 @@ K_PASS = 4 * P
 PASSES = N // K_PASS
 AHEAD = 3
 QUANTISE_LAG = 1
-FINISH_LAG = 6
+FINISH_LAG = 3
 SIGN_COLUMNS = 1536
+WINDOW_TILE = FINISH_LAG + 2
 UNSIGNED_TILES = 2
 EXP_CAP = 3.0e38
 
@@ -46,6 +47,7 @@ def tile_patternlayer_t_v_kernel(tc, inputs, train_data, dist, grad_out, out):
         stage = stack.enter_context(tc.tile_pool(name="stage", bufs=2))
         waiting = stack.enter_context(tc.tile_pool(name="waiting", bufs=QUANTISE_LAG + 1))
         small = stack.enter_context(tc.tile_pool(name="small", bufs=FINISH_LAG + 1))
+        tests = stack.enter_context(tc.tile_pool(name="tests", bufs=1))
         signs = stack.enter_context(tc.tile_pool(name="signs", bufs=3))
         results = stack.enter_context(tc.tile_pool(name="results", bufs=FINISH_LAG))
         flipped = stack.enter_context(tc.psum_pool(name="flipped", bufs=2))
@@ -53,7 +55,7 @@ def tile_patternlayer_t_v_kernel(tc, inputs, train_data, dist, grad_out, out):
 
         z_of, g_of, x_of, prob_of, e_of, r_of = {}, {}, {}, {}, {}, {}
         banks_of, grouped_of, codes_of, scales_of, acc_of, g_kept_of = {}, {}, {}, {}, {}, {}
-        z_sign_of = {}
+        z_sign_of, test_of = {}, {}
 
         def load(i, parts=1):
             z = loads.tile([P, N], F32)
@@ -81,6 +83,13 @@ def tile_patternlayer_t_v_kernel(tc, inputs, train_data, dist, grad_out, out):
             nc.scalar.activation(out=z_sign[:], in_=z_of[i][:, :SIGN_COLUMNS], func=ACT.Sign)
             z_sign_of[i] = z_sign
 
+        def window_test(i):
+            test = tests.tile([P, N - SIGN_COLUMNS], BF16)
+            nc.gpsimd.tensor_scalar(
+                out=test[:], in0=z_of[i][:, SIGN_COLUMNS:], scalar1=0.0, scalar2=1.0, op0=ALU.is_gt, op1=ALU.mult
+            )
+            test_of[i] = test
+
         def mask_on_vector(i, parts):
             g_kept = stage.tile([P, N], BF16)
             for h in range(parts):
@@ -99,14 +108,19 @@ def tile_patternlayer_t_v_kernel(tc, inputs, train_data, dist, grad_out, out):
             g_kept = stage.tile([P, N], BF16)
             z_sign = z_sign_of[i]
             nc.vector.tensor_scalar_max(out=z_sign[:], in0=z_sign[:], scalar1=0.0)
-            nc.vector.scalar_tensor_tensor(
-                out=g_kept[:, SIGN_COLUMNS:],
-                in0=z_of[i][:, SIGN_COLUMNS:],
-                scalar=0.0,
-                in1=g_of[i][:, SIGN_COLUMNS:],
-                op0=ALU.is_gt,
-                op1=ALU.mult,
-            )
+            if i >= WINDOW_TILE:
+                nc.vector.tensor_tensor(
+                    out=g_kept[:, SIGN_COLUMNS:], in0=test_of[i][:], in1=g_of[i][:, SIGN_COLUMNS:], op=ALU.mult
+                )
+            else:
+                nc.vector.scalar_tensor_tensor(
+                    out=g_kept[:, SIGN_COLUMNS:],
+                    in0=z_of[i][:, SIGN_COLUMNS:],
+                    scalar=0.0,
+                    in1=g_of[i][:, SIGN_COLUMNS:],
+                    op0=ALU.is_gt,
+                    op1=ALU.mult,
+                )
             nc.vector.tensor_tensor(
                 out=g_kept[:, :SIGN_COLUMNS], in0=z_sign[:], in1=g_of[i][:, :SIGN_COLUMNS], op=ALU.mult
             )
@@ -241,6 +255,8 @@ def tile_patternlayer_t_v_kernel(tc, inputs, train_data, dist, grad_out, out):
                     mask(s + 1)
             if s == 1:
                 quantise_train(3)
+            if WINDOW_TILE <= s + 2 < ROW_TILES:
+                window_test(s + 2)
             if s >= FINISH_LAG:
                 finish(s - FINISH_LAG)
             if 0 <= s - QUANTISE_LAG < ROW_TILES:

@@ -23,8 +23,10 @@ AHEAD = 3
 QUANTISE_LAG = 1
 FINISH_LAG = 3
 SIGN_COLUMNS = 1536
+TEST_COLUMNS = 384
+TEST_FROM = N - TEST_COLUMNS
 WINDOW_TILE = FINISH_LAG + 2
-UNSIGNED_TILES = 2
+UNSIGNED_TILES = 3
 EXP_CAP = 3.0e38
 
 FLOPS = 2 * B * N * D
@@ -84,9 +86,9 @@ def tile_patternlayer_t_v_kernel(tc, inputs, train_data, dist, grad_out, out):
             z_sign_of[i] = z_sign
 
         def window_test(i):
-            test = tests.tile([P, N - SIGN_COLUMNS], BF16)
+            test = tests.tile([P, TEST_COLUMNS], BF16)
             nc.gpsimd.tensor_scalar(
-                out=test[:], in0=z_of[i][:, SIGN_COLUMNS:], scalar1=0.0, scalar2=1.0, op0=ALU.is_gt, op1=ALU.mult
+                out=test[:], in0=z_of[i][:, TEST_FROM:], scalar1=0.0, scalar2=1.0, op0=ALU.is_gt, op1=ALU.mult
             )
             test_of[i] = test
 
@@ -108,31 +110,39 @@ def tile_patternlayer_t_v_kernel(tc, inputs, train_data, dist, grad_out, out):
             g_kept = stage.tile([P, N], BF16)
             z_sign = z_sign_of[i]
             nc.vector.tensor_scalar_max(out=z_sign[:], in0=z_sign[:], scalar1=0.0)
+            vector_to = TEST_FROM if i >= WINDOW_TILE else N
             if i >= WINDOW_TILE:
                 nc.vector.tensor_tensor(
-                    out=g_kept[:, SIGN_COLUMNS:], in0=test_of[i][:], in1=g_of[i][:, SIGN_COLUMNS:], op=ALU.mult
+                    out=g_kept[:, TEST_FROM:], in0=test_of[i][:], in1=g_of[i][:, TEST_FROM:], op=ALU.mult
                 )
-            else:
-                nc.vector.scalar_tensor_tensor(
-                    out=g_kept[:, SIGN_COLUMNS:],
-                    in0=z_of[i][:, SIGN_COLUMNS:],
-                    scalar=0.0,
-                    in1=g_of[i][:, SIGN_COLUMNS:],
-                    op0=ALU.is_gt,
-                    op1=ALU.mult,
-                )
+            nc.vector.scalar_tensor_tensor(
+                out=g_kept[:, SIGN_COLUMNS:vector_to],
+                in0=z_of[i][:, SIGN_COLUMNS:vector_to],
+                scalar=0.0,
+                in1=g_of[i][:, SIGN_COLUMNS:vector_to],
+                op0=ALU.is_gt,
+                op1=ALU.mult,
+            )
             nc.vector.tensor_tensor(
                 out=g_kept[:, :SIGN_COLUMNS], in0=z_sign[:], in1=g_of[i][:, :SIGN_COLUMNS], op=ALU.mult
             )
             g_kept_of[i] = g_kept
 
-        def weigh(i):
+        def weigh(i, parts):
             e = stage.tile([P, N], BF16)
-            r = small.tile([P, 1], F32)
-            nc.vector.scalar_tensor_tensor(
-                out=e[:], in0=prob_of[i][:], scalar=EXP_CAP, in1=g_kept_of[i][:], op0=ALU.min, op1=ALU.mult, accum_out=r[:]
-            )
+            r = small.tile([P, 2], F32)
             e_of[i], r_of[i] = e, r
+            for h in range(parts):
+                cols = slice(h * (N // parts), (h + 1) * (N // parts))
+                nc.vector.scalar_tensor_tensor(
+                    out=e[:, cols],
+                    in0=prob_of[i][:, cols],
+                    scalar=EXP_CAP,
+                    in1=g_kept_of[i][:, cols],
+                    op0=ALU.min,
+                    op1=ALU.mult,
+                    accum_out=r[:, h : h + 1],
+                )
 
         def flip(i):
             e_words = e_of[i][:].bitcast(F32)
@@ -155,14 +165,16 @@ def tile_patternlayer_t_v_kernel(tc, inputs, train_data, dist, grad_out, out):
                 )
             grouped_of[i] = e_grouped
 
-        def quantise(i):
+        def quantise(i, parts):
             e_codes = stage.tile([P, PASSES, P], U32, align_bytes=64)
             e_scales = stage.tile([P, PASSES, P], U8, align_bytes=64)
-            nc.vector.quantize_mx(
-                out=e_codes[:].rearrange("p c b -> p (c b)").bitcast(E5M2X4),
-                scales=e_scales[:].rearrange("p c b -> p (c b)"),
-                in_=grouped_of[i][:].rearrange("p c b t -> p (c b t)"),
-            )
+            for h in range(parts):
+                passes = slice(h * (PASSES // parts), (h + 1) * (PASSES // parts))
+                nc.vector.quantize_mx(
+                    out=e_codes[:, passes].rearrange("p c b -> p (c b)").bitcast(E5M2X4),
+                    scales=e_scales[:, passes].rearrange("p c b -> p (c b)"),
+                    in_=grouped_of[i][:, passes].rearrange("p c b t -> p (c b t)"),
+                )
             codes_of[i], scales_of[i] = e_codes, e_scales
 
         def multiply(i):
@@ -244,8 +256,11 @@ def tile_patternlayer_t_v_kernel(tc, inputs, train_data, dist, grad_out, out):
             if s + 2 < ROW_TILES:
                 sign(s + 2)
             if s < ROW_TILES:
-                weigh(s)
+                weigh(s, parts=2 if s == ROW_TILES - 1 else 1)
                 flip(s)
+                if s == ROW_TILES - 1:
+                    r_last = r_of[s]
+                    nc.gpsimd.tensor_tensor(out=r_last[:, 0:1], in0=r_last[:, 0:1], in1=r_last[:, 1:2], op=ALU.add)
             if s == 0:
                 quantise_train(2)
             if s + 1 < ROW_TILES:
@@ -260,5 +275,5 @@ def tile_patternlayer_t_v_kernel(tc, inputs, train_data, dist, grad_out, out):
             if s >= FINISH_LAG:
                 finish(s - FINISH_LAG)
             if 0 <= s - QUANTISE_LAG < ROW_TILES:
-                quantise(s - QUANTISE_LAG)
+                quantise(s - QUANTISE_LAG, parts=2 if s - QUANTISE_LAG == ROW_TILES - 1 else 1)
                 multiply(s - QUANTISE_LAG)

@@ -111,10 +111,6 @@ def tile_patternlayer_t_v_kernel(tc, inputs, train_data, dist, grad_out, out):
             z_sign = z_sign_of[i]
             nc.vector.tensor_scalar_max(out=z_sign[:], in0=z_sign[:], scalar1=0.0)
             vector_to = TEST_FROM if i >= WINDOW_TILE else N
-            if i >= WINDOW_TILE:
-                nc.vector.tensor_tensor(
-                    out=g_kept[:, TEST_FROM:], in0=test_of[i][:], in1=g_of[i][:, TEST_FROM:], op=ALU.mult
-                )
             nc.vector.scalar_tensor_tensor(
                 out=g_kept[:, SIGN_COLUMNS:vector_to],
                 in0=z_of[i][:, SIGN_COLUMNS:vector_to],
@@ -123,6 +119,10 @@ def tile_patternlayer_t_v_kernel(tc, inputs, train_data, dist, grad_out, out):
                 op0=ALU.is_gt,
                 op1=ALU.mult,
             )
+            if i >= WINDOW_TILE:
+                nc.vector.tensor_tensor(
+                    out=g_kept[:, TEST_FROM:], in0=test_of[i][:], in1=g_of[i][:, TEST_FROM:], op=ALU.mult
+                )
             nc.vector.tensor_tensor(
                 out=g_kept[:, :SIGN_COLUMNS], in0=z_sign[:], in1=g_of[i][:, :SIGN_COLUMNS], op=ALU.mult
             )

@@ -20,14 +20,18 @@ ROW_TILES = B // P
 K_PASS = 4 * P
 PASSES = N // K_PASS
 AHEAD = 3
-QUANTISE_LAG = 1
 FINISH_LAG = 3
 SIGN_COLUMNS = 1536
 TEST_COLUMNS = 384
 TEST_FROM = N - TEST_COLUMNS
+HELD_BACK = 2
 WINDOW_TILE = FINISH_LAG + 2
 UNSIGNED_TILES = 3
 EXP_CAP = 3.0e38
+
+ALL = slice(0, D)
+LEFT = slice(0, D // 2)
+RIGHT = slice(D // 2, D)
 
 FLOPS = 2 * B * N * D
 
@@ -39,7 +43,7 @@ def tile_patternlayer_t_v_kernel(tc, inputs, train_data, dist, grad_out, out):
     grad_tiles = grad_out.rearrange("(p i) n -> i p n", i=ROW_TILES)
     x_tiles = inputs.rearrange("(p i) d -> i p d", i=ROW_TILES)
     out_tiles = out.rearrange("(p i) d -> i p d", i=ROW_TILES)
-    train_passes = train_data.rearrange("(c u p e) d -> c p u (e d)", c=PASSES, u=2, p=P, e=2)
+    train_passes = train_data.rearrange("(c u p e) d -> c u p e d", c=PASSES, u=2, p=P, e=2)
 
     with ExitStack() as stack:
         stack.enter_context(tc.manual_schedule())
@@ -47,13 +51,13 @@ def tile_patternlayer_t_v_kernel(tc, inputs, train_data, dist, grad_out, out):
         loads = stack.enter_context(tc.tile_pool(name="loads", bufs=AHEAD + 1))
         x_pool = stack.enter_context(tc.tile_pool(name="x_pool", bufs=AHEAD + FINISH_LAG + 1))
         stage = stack.enter_context(tc.tile_pool(name="stage", bufs=2))
-        waiting = stack.enter_context(tc.tile_pool(name="waiting", bufs=QUANTISE_LAG + 1))
-        small = stack.enter_context(tc.tile_pool(name="small", bufs=FINISH_LAG + 1))
+        waiting = stack.enter_context(tc.tile_pool(name="waiting", bufs=2))
+        small = stack.enter_context(tc.tile_pool(name="small", bufs=FINISH_LAG + HELD_BACK + 1))
         tests = stack.enter_context(tc.tile_pool(name="tests", bufs=1))
         signs = stack.enter_context(tc.tile_pool(name="signs", bufs=3))
-        results = stack.enter_context(tc.tile_pool(name="results", bufs=FINISH_LAG))
+        results = stack.enter_context(tc.tile_pool(name="results", bufs=FINISH_LAG + HELD_BACK))
         flipped = stack.enter_context(tc.psum_pool(name="flipped", bufs=2))
-        sums = stack.enter_context(tc.psum_pool(name="sums", bufs=FINISH_LAG - QUANTISE_LAG + 1))
+        sums = stack.enter_context(tc.psum_pool(name="sums", bufs=FINISH_LAG + HELD_BACK))
 
         z_of, g_of, x_of, prob_of, e_of, r_of = {}, {}, {}, {}, {}, {}
         banks_of, grouped_of, codes_of, scales_of, acc_of, g_kept_of = {}, {}, {}, {}, {}, {}
@@ -92,9 +96,11 @@ def tile_patternlayer_t_v_kernel(tc, inputs, train_data, dist, grad_out, out):
             )
             test_of[i] = test
 
-        def mask_on_vector(i, parts):
+        def mask_on_vector(i, parts, between=None):
             g_kept = stage.tile([P, N], BF16)
             for h in range(parts):
+                if h > 0 and between is not None:
+                    between()
                 cols = slice(h * (N // parts), (h + 1) * (N // parts))
                 nc.vector.scalar_tensor_tensor(
                     out=g_kept[:, cols],
@@ -191,18 +197,24 @@ def tile_patternlayer_t_v_kernel(tc, inputs, train_data, dist, grad_out, out):
                 )
             acc_of[i] = acc
 
-        def finish(i):
+        def finish(i, parts=1):
             result = results.tile([P, D], F32)
-            nc.vector.scalar_tensor_tensor(
-                out=result[:],
-                in0=x_of[i][:],
-                scalar=r_of[i][:, 0:1],
-                in1=acc_of[i][:],
-                op0=ALU.mult,
-                op1=ALU.subtract,
-                reverse1=True,
-            )
-            nc.sync.dma_start(out=out_tiles[i], in_=result[:])
+            for h in range(parts):
+                cols = slice(h * (D // parts), (h + 1) * (D // parts))
+                nc.vector.scalar_tensor_tensor(
+                    out=result[:, cols],
+                    in0=x_of[i][:, cols],
+                    scalar=r_of[i][:, 0:1],
+                    in1=acc_of[i][:, cols],
+                    op0=ALU.mult,
+                    op1=ALU.subtract,
+                    reverse1=True,
+                )
+                nc.sync.dma_start(out=out_tiles[i][:, cols], in_=result[:, cols])
+
+        first = keep.tile([P, 1], F32)
+        nc.gpsimd.memset(first[:], 0.0)
+        nc.scalar.activation(out=first[:], in_=first[:], func=ACT.Exp)
 
         identity = keep.tile([P, P], F32)
         make_identity(nc, identity[:])
@@ -211,11 +223,12 @@ def tile_patternlayer_t_v_kernel(tc, inputs, train_data, dist, grad_out, out):
         t_grouped = keep.tile([P, PASSES, D, 4], BF16, align_bytes=64)
         t_codes = keep.tile([P, PASSES, D], U32, align_bytes=64)
         t_scales = keep.tile([P, PASSES, D], U8, align_bytes=64)
-        def load_train(c):
-            nc.sync.dma_start(out=t_raw[:, c].rearrange("p (u e) d -> p u (e d)", u=2), in_=train_passes[c])
+        def load_train(c, cols=ALL):
+            for u in range(2):
+                nc.sync.dma_start(out=t_raw[:, c, 2 * u : 2 * u + 2, cols], in_=train_passes[c, u][:, :, cols])
 
-        def regroup_train(engine_copy, c):
-            engine_copy(out=t_grouped[:, c], in_=t_raw[:, c].rearrange("p t d -> p d t"))
+        def regroup_train(engine_copy, c, cols=ALL):
+            engine_copy(out=t_grouped[:, c, cols], in_=t_raw[:, c, :, cols].rearrange("p t d -> p d t"))
 
         def quantise_train(c):
             nc.vector.quantize_mx(
@@ -224,35 +237,34 @@ def tile_patternlayer_t_v_kernel(tc, inputs, train_data, dist, grad_out, out):
                 in_=t_grouped[:, c].rearrange("p d t -> p (d t)"),
             )
 
-        load_train(0)
+        load_train(0, LEFT)
+        load_train(0, RIGHT)
         load_train(1)
         load(0, parts=2)
-        load_train(2)
         load(1)
+        load_train(2)
         load_train(3)
         load(2)
         for i in range(AHEAD):
             load_x(i)
 
-        regroup_train(nc.vector.tensor_copy, 0)
-        regroup_train(nc.vector.tensor_copy, 1)
+        for c in range(2):
+            regroup_train(nc.vector.tensor_copy, c, LEFT)
+            regroup_train(nc.scalar.copy, c, RIGHT)
         quantise_train(0)
-        quantise_train(1)
         exponential(0, parts=2)
-        mask_on_vector(0, parts=2)
-        regroup_train(nc.scalar.copy, 2)
-        for s in range(ROW_TILES + FINISH_LAG):
+        mask_on_vector(0, parts=2, between=lambda: quantise_train(1))
+        for s in range(ROW_TILES):
             if s + AHEAD < ROW_TILES:
                 load(s + AHEAD)
                 load_x(s + AHEAD)
-            if s == 0:
-                exponential(1)
-            if 1 <= s <= ROW_TILES:
+            if s >= 1:
                 regroup(s - 1)
-            if s == 0:
-                regroup_train(nc.scalar.copy, 3)
-            if 1 <= s and s + 1 < ROW_TILES:
+            if s + 1 < ROW_TILES:
                 exponential(s + 1)
+            if s == 0:
+                regroup_train(nc.scalar.copy, 2)
+                regroup_train(nc.scalar.copy, 3)
             if s + 2 < ROW_TILES:
                 sign(s + 2)
             if s < ROW_TILES:
@@ -261,7 +273,7 @@ def tile_patternlayer_t_v_kernel(tc, inputs, train_data, dist, grad_out, out):
                 if s == ROW_TILES - 1:
                     r_last = r_of[s]
                     nc.gpsimd.tensor_tensor(out=r_last[:, 0:1], in0=r_last[:, 0:1], in1=r_last[:, 1:2], op=ALU.add)
-            if s == 0:
+            if s == 1:
                 quantise_train(2)
             if s + 1 < ROW_TILES:
                 if s + 1 < UNSIGNED_TILES:
@@ -272,8 +284,18 @@ def tile_patternlayer_t_v_kernel(tc, inputs, train_data, dist, grad_out, out):
                 quantise_train(3)
             if WINDOW_TILE <= s + 2 < ROW_TILES:
                 window_test(s + 2)
-            if s >= FINISH_LAG:
+            if FINISH_LAG <= s < ROW_TILES - HELD_BACK:
                 finish(s - FINISH_LAG)
-            if 0 <= s - QUANTISE_LAG < ROW_TILES:
-                quantise(s - QUANTISE_LAG, parts=2 if s - QUANTISE_LAG == ROW_TILES - 1 else 1)
-                multiply(s - QUANTISE_LAG)
+            if s >= 1:
+                quantise(s - 1, parts=1)
+                multiply(s - 1)
+
+        last = ROW_TILES - 1
+        regroup(last)
+        finish(last - 4)
+        finish(last - 3)
+        quantise(last, parts=2)
+        multiply(last)
+        finish(last - 2)
+        finish(last - 1)
+        finish(last, parts=2)

@@ -212,6 +212,18 @@ def tile_patternlayer_t_v_kernel(tc, inputs, train_data, dist, grad_out, out):
                 )
                 nc.sync.dma_start(out=out_tiles[i][:, cols], in_=result[:, cols])
 
+        def row_product(i):
+            product = keep.tile([P, D], F32)
+            nc.scalar.activation(out=product[:], in_=x_of[i][:], func=ACT.Copy, scale=r_of[i][:, 0:1])
+            return product
+
+        def finish_on_others(i, product):
+            acc_sbuf = keep.tile([P, D], F32)
+            nc.scalar.copy(out=acc_sbuf[:], in_=acc_of[i][:])
+            result = results.tile([P, D], F32)
+            nc.gpsimd.tensor_tensor(out=result[:], in0=acc_sbuf[:], in1=product[:], op=ALU.subtract)
+            nc.scalar.dma_start(out=out_tiles[i], in_=result[:])
+
         first = keep.tile([P, 1], F32)
         nc.gpsimd.memset(first[:], 0.0)
         nc.scalar.activation(out=first[:], in_=first[:], func=ACT.Exp)
@@ -228,7 +240,10 @@ def tile_patternlayer_t_v_kernel(tc, inputs, train_data, dist, grad_out, out):
                 nc.sync.dma_start(out=t_raw[:, c, 2 * u : 2 * u + 2, cols], in_=train_passes[c, u][:, :, cols])
 
         def regroup_train(engine_copy, c, cols=ALL):
-            engine_copy(out=t_grouped[:, c, cols], in_=t_raw[:, c, :, cols].rearrange("p t d -> p d t"))
+            engine_copy(
+                out=t_grouped[:, c, cols].rearrange("p (d i) t -> p d t i", i=4),
+                in_=t_raw[:, c, :, cols].rearrange("p t (d i) -> p d t i", i=4),
+            )
 
         def quantise_train(c):
             nc.vector.quantize_mx(
@@ -265,14 +280,11 @@ def tile_patternlayer_t_v_kernel(tc, inputs, train_data, dist, grad_out, out):
             if s == 0:
                 regroup_train(nc.scalar.copy, 2)
                 regroup_train(nc.scalar.copy, 3)
-            if s + 2 < ROW_TILES:
+            if UNSIGNED_TILES <= s + 2 < ROW_TILES:
                 sign(s + 2)
             if s < ROW_TILES:
                 weigh(s, parts=2 if s == ROW_TILES - 1 else 1)
                 flip(s)
-                if s == ROW_TILES - 1:
-                    r_last = r_of[s]
-                    nc.gpsimd.tensor_tensor(out=r_last[:, 0:1], in0=r_last[:, 0:1], in1=r_last[:, 1:2], op=ALU.add)
             if s == 1:
                 quantise_train(2)
             if s + 1 < ROW_TILES:
@@ -291,11 +303,14 @@ def tile_patternlayer_t_v_kernel(tc, inputs, train_data, dist, grad_out, out):
                 multiply(s - 1)
 
         last = ROW_TILES - 1
+        r_last = r_of[last]
+        nc.gpsimd.tensor_tensor(out=r_last[:, 0:1], in0=r_last[:, 0:1], in1=r_last[:, 1:2], op=ALU.add)
+        product = row_product(last - 2)
         regroup(last)
         finish(last - 4)
         finish(last - 3)
         quantise(last, parts=2)
         multiply(last)
-        finish(last - 2)
+        finish_on_others(last - 2, product)
         finish(last - 1)
         finish(last, parts=2)

from contextlib import ExitStack

import concourse.mybir as mybir
from concourse.masks import make_identity

F32 = mybir.dt.float32
BF16 = mybir.dt.bfloat16
U32 = mybir.dt.uint32
U8 = mybir.dt.uint8
E5M2X4 = mybir.dt.float8_e5m2_x4
E4M3X4 = mybir.dt.float8_e4m3fn_x4
ALU = mybir.AluOpType
ACT = mybir.ActivationFunctionType

P = 128
B = 2048
N = 2048
D = 512
ROW_TILES = B // P
K_PASS = 4 * P
PASSES = N // K_PASS
AHEAD = 3
FINISH_LAG = 3
SIGN_COLUMNS = 1536
TEST_COLUMNS = 384
TEST_FROM = N - TEST_COLUMNS
HELD_BACK = 2
WINDOW_TILE = FINISH_LAG + 2
UNSIGNED_TILES = 3
EXP_CAP = 3.0e38

ALL = slice(0, D)
LEFT = slice(0, D // 2)
RIGHT = slice(D // 2, D)

FLOPS = 2 * B * N * D


def tile_patternlayer_t_v_kernel(tc, inputs, train_data, dist, grad_out, out):
    nc = tc.nc

    dist_tiles = dist.rearrange("(p i) n -> i p n", i=ROW_TILES)
    grad_tiles = grad_out.rearrange("(p i) n -> i p n", i=ROW_TILES)
    x_tiles = inputs.rearrange("(p i) d -> i p d", i=ROW_TILES)
    out_tiles = out.rearrange("(p i) d -> i p d", i=ROW_TILES)
    train_passes = train_data.rearrange("(c u p e) d -> c u p e d", c=PASSES, u=2, p=P, e=2)

    with ExitStack() as stack:
        stack.enter_context(tc.manual_schedule())
        keep = stack.enter_context(tc.tile_pool(name="keep", bufs=1))
        loads = stack.enter_context(tc.tile_pool(name="loads", bufs=AHEAD + 1))
        x_pool = stack.enter_context(tc.tile_pool(name="x_pool", bufs=AHEAD + FINISH_LAG + 1))
        stage = stack.enter_context(tc.tile_pool(name="stage", bufs=2))
        waiting = stack.enter_context(tc.tile_pool(name="waiting", bufs=2))
        small = stack.enter_context(tc.tile_pool(name="small", bufs=FINISH_LAG + HELD_BACK + 1))
        tests = stack.enter_context(tc.tile_pool(name="tests", bufs=1))
        signs = stack.enter_context(tc.tile_pool(name="signs", bufs=3))
        results = stack.enter_context(tc.tile_pool(name="results", bufs=FINISH_LAG + HELD_BACK))
        flipped = stack.enter_context(tc.psum_pool(name="flipped", bufs=2))
        sums = stack.enter_context(tc.psum_pool(name="sums", bufs=FINISH_LAG + HELD_BACK))

        z_of, g_of, x_of, prob_of, e_of, r_of = {}, {}, {}, {}, {}, {}
        banks_of, grouped_of, codes_of, scales_of, acc_of, g_kept_of = {}, {}, {}, {}, {}, {}
        z_sign_of, test_of = {}, {}

        def load(i, parts=1):
            z = loads.tile([P, N], F32)
            g = loads.tile([P, N], BF16)
            for h in range(parts):
                cols = slice(h * (N // parts), (h + 1) * (N // parts))
                nc.sync.dma_start(out=z[:, cols], in_=dist_tiles[i][:, cols])
                nc.sync.dma_start(out=g[:, cols], in_=grad_tiles[i][:, cols])
            z_of[i], g_of[i] = z, g

        def load_x(i):
            x = x_pool.tile([P, D], BF16)
            nc.sync.dma_start(out=x[:], in_=x_tiles[i])
            x_of[i] = x

        def exponential(i, parts=1):
            prob = stage.tile([P, N], F32)
            for h in range(parts):
                cols = slice(h * (N // parts), (h + 1) * (N // parts))
                nc.scalar.activation(out=prob[:, cols], in_=z_of[i][:, cols], func=ACT.Exp, scale=-0.5)
            prob_of[i] = prob

        def sign(i):
            z_sign = signs.tile([P, SIGN_COLUMNS], BF16)
            nc.scalar.activation(out=z_sign[:], in_=z_of[i][:, :SIGN_COLUMNS], func=ACT.Sign)
            z_sign_of[i] = z_sign

        def window_test(i):
            test = tests.tile([P, TEST_COLUMNS], BF16)
            nc.gpsimd.tensor_scalar(
                out=test[:], in0=z_of[i][:, TEST_FROM:], scalar1=0.0, scalar2=1.0, op0=ALU.is_gt, op1=ALU.mult
            )
            test_of[i] = test

        def mask_on_vector(i, parts, between=None):
            g_kept = stage.tile([P, N], BF16)
            for h in range(parts):
                if h > 0 and between is not None:
                    between()
                cols = slice(h * (N // parts), (h + 1) * (N // parts))
                nc.vector.scalar_tensor_tensor(
                    out=g_kept[:, cols],
                    in0=z_of[i][:, cols],
                    scalar=0.0,
                    in1=g_of[i][:, cols],
                    op0=ALU.is_gt,
                    op1=ALU.mult,
                )
            g_kept_of[i] = g_kept

        def mask(i):
            g_kept = stage.tile([P, N], BF16)
            z_sign = z_sign_of[i]
            nc.vector.tensor_scalar_max(out=z_sign[:], in0=z_sign[:], scalar1=0.0)
            vector_to = TEST_FROM if i >= WINDOW_TILE else N
            nc.vector.scalar_tensor_tensor(
                out=g_kept[:, SIGN_COLUMNS:vector_to],
                in0=z_of[i][:, SIGN_COLUMNS:vector_to],
                scalar=0.0,
                in1=g_of[i][:, SIGN_COLUMNS:vector_to],
                op0=ALU.is_gt,
                op1=ALU.mult,
            )
            if i >= WINDOW_TILE:
                nc.vector.tensor_tensor(
                    out=g_kept[:, TEST_FROM:], in0=test_of[i][:], in1=g_of[i][:, TEST_FROM:], op=ALU.mult
                )
            nc.vector.tensor_tensor(
                out=g_kept[:, :SIGN_COLUMNS], in0=z_sign[:], in1=g_of[i][:, :SIGN_COLUMNS], op=ALU.mult
            )
            g_kept_of[i] = g_kept

        def weigh(i, parts):
            e = stage.tile([P, N], BF16)
            r = small.tile([P, 2], F32)
            e_of[i], r_of[i] = e, r
            for h in range(parts):
                cols = slice(h * (N // parts), (h + 1) * (N // parts))
                nc.vector.scalar_tensor_tensor(
                    out=e[:, cols],
                    in0=prob_of[i][:, cols],
                    scalar=EXP_CAP,
                    in1=g_kept_of[i][:, cols],
                    op0=ALU.min,
                    op1=ALU.mult,
                    accum_out=r[:, h : h + 1],
                )

        def flip(i):
            e_words = e_of[i][:].bitcast(F32)
            banks_of[i] = []
            for h in range(PASSES // 2):
                bank = flipped.tile([P, 2, 2, P], F32)
                for c in range(2):
                    for u in range(2):
                        w0 = P * (4 * h + 2 * c + u)
                        nc.tensor.transpose(bank[:, c, u, :], e_words[:, w0 : w0 + P], identity[:])
                banks_of[i].append(bank)

        def regroup(i):
            e_grouped = waiting.tile([P, PASSES, P, 4], BF16, align_bytes=64)
            e_grouped_words = e_grouped[:].bitcast(F32)
            for h in range(PASSES // 2):
                nc.scalar.copy(
                    out=e_grouped_words[:, 2 * h : 2 * h + 2, :, :],
                    in_=banks_of[i][h][:].rearrange("p c u b -> p c b u"),
                )
            grouped_of[i] = e_grouped

        def quantise(i, parts):
            e_codes = stage.tile([P, PASSES, P], U32, align_bytes=64)
            e_scales = stage.tile([P, PASSES, P], U8, align_bytes=64)
            for h in range(parts):
                passes = slice(h * (PASSES // parts), (h + 1) * (PASSES // parts))
                nc.vector.quantize_mx(
                    out=e_codes[:, passes].rearrange("p c b -> p (c b)").bitcast(E5M2X4),
                    scales=e_scales[:, passes].rearrange("p c b -> p (c b)"),
                    in_=grouped_of[i][:, passes].rearrange("p c b t -> p (c b t)"),
                )
            codes_of[i], scales_of[i] = e_codes, e_scales

        def multiply(i):
            acc = sums.tile([P, D], F32)
            for c in range(PASSES):
                nc.tensor.matmul_mx(
                    out=acc[:],
                    lhsT=codes_of[i][:, c, :].bitcast(E5M2X4),
                    lhsT_scale=scales_of[i][:, c, :],
                    rhs=t_codes[:, c, :].bitcast(E4M3X4),
                    rhs_scale=t_scales[:, c, :],
                    start=(c == 0),
                    stop=(c == PASSES - 1),
                )
            acc_of[i] = acc

        def finish(i, parts=1):
            result = results.tile([P, D], F32)
            for h in range(parts):
                cols = slice(h * (D // parts), (h + 1) * (D // parts))
                nc.vector.scalar_tensor_tensor(
                    out=result[:, cols],
                    in0=x_of[i][:, cols],
                    scalar=r_of[i][:, 0:1],
                    in1=acc_of[i][:, cols],
                    op0=ALU.mult,
                    op1=ALU.subtract,
                    reverse1=True,
                )
                nc.sync.dma_start(out=out_tiles[i][:, cols], in_=result[:, cols])

        def row_product(i):
            product = keep.tile([P, D], F32)
            nc.scalar.activation(out=product[:], in_=x_of[i][:], func=ACT.Copy, scale=r_of[i][:, 0:1])
            return product

        def finish_on_others(i, product):
            acc_sbuf = keep.tile([P, D], F32)
            nc.scalar.copy(out=acc_sbuf[:], in_=acc_of[i][:])
            result = results.tile([P, D], F32)
            nc.gpsimd.tensor_tensor(out=result[:], in0=acc_sbuf[:], in1=product[:], op=ALU.subtract)
            nc.scalar.dma_start(out=out_tiles[i], in_=result[:])

        first = keep.tile([P, 1], F32)
        nc.gpsimd.memset(first[:], 0.0)
        nc.scalar.activation(out=first[:], in_=first[:], func=ACT.Exp)

        identity = keep.tile([P, P], F32)
        make_identity(nc, identity[:])

        t_raw = keep.tile([P, PASSES, 4, D], BF16)
        t_grouped = keep.tile([P, PASSES, D, 4], BF16, align_bytes=64)
        t_codes = keep.tile([P, PASSES, D], U32, align_bytes=64)
        t_scales = keep.tile([P, PASSES, D], U8, align_bytes=64)
        def load_train(c, cols=ALL):
            for u in range(2):
                nc.sync.dma_start(out=t_raw[:, c, 2 * u : 2 * u + 2, cols], in_=train_passes[c, u][:, :, cols])

        def regroup_train(engine_copy, c, cols=ALL):
            engine_copy(
                out=t_grouped[:, c, cols].rearrange("p (d i) t -> p d t i", i=4),
                in_=t_raw[:, c, :, cols].rearrange("p t (d i) -> p d t i", i=4),
            )

        def quantise_train(c):
            nc.vector.quantize_mx(
                out=t_codes[:, c, :].bitcast(E4M3X4),
                scales=t_scales[:, c, :],
                in_=t_grouped[:, c].rearrange("p d t -> p (d t)"),
            )

        load_train(0, LEFT)
        load_train(0, RIGHT)
        load_train(1)
        load(0, parts=2)
        load(1)
        load_train(2)
        load_train(3)
        load(2)
        for i in range(AHEAD):
            load_x(i)

        for c in range(2):
            regroup_train(nc.vector.tensor_copy, c, LEFT)
            regroup_train(nc.scalar.copy, c, RIGHT)
        quantise_train(0)
        exponential(0, parts=2)
        mask_on_vector(0, parts=2, between=lambda: quantise_train(1))
        for s in range(ROW_TILES):
            if s + AHEAD < ROW_TILES:
                load(s + AHEAD)
                load_x(s + AHEAD)
            if s >= 1:
                regroup(s - 1)
            if s + 1 < ROW_TILES:
                exponential(s + 1)
            if s == 0:
                regroup_train(nc.scalar.copy, 2)
                regroup_train(nc.scalar.copy, 3)
            if UNSIGNED_TILES <= s + 2 < ROW_TILES:
                sign(s + 2)
            if s < ROW_TILES:
                weigh(s, parts=2 if s == ROW_TILES - 1 else 1)
                flip(s)
            if s == 1:
                quantise_train(2)
            if s + 1 < ROW_TILES:
                if s + 1 < UNSIGNED_TILES:
                    mask_on_vector(s + 1, parts=1)
                else:
                    mask(s + 1)
            if s == 1:
                quantise_train(3)
            if WINDOW_TILE <= s + 2 < ROW_TILES:
                window_test(s + 2)
            if FINISH_LAG <= s < ROW_TILES - HELD_BACK:
                finish(s - FINISH_LAG)
            if s >= 1:
                quantise(s - 1, parts=1)
                multiply(s - 1)

        last = ROW_TILES - 1
        r_last = r_of[last]
        nc.gpsimd.tensor_tensor(out=r_last[:, 0:1], in0=r_last[:, 0:1], in1=r_last[:, 1:2], op=ALU.add)
        product = row_product(last - 2)
        regroup(last)
        finish(last - 4)
        finish(last - 3)
        quantise(last, parts=2)
        multiply(last)
        finish_on_others(last - 2, product)
        finish(last - 1)
        finish(last, parts=2)
